import numpy as np
import ml_dtypes


def mxq(x, axis, fmt="e4m3"):
    dtype, down = {"e4m3": (ml_dtypes.float8_e4m3fn, 7), "e5m2": (ml_dtypes.float8_e5m2, 14)}[fmt]
    v = np.moveaxis(np.asarray(x, np.float32).astype(ml_dtypes.bfloat16).astype(np.float64), axis, -1)
    blocks = v.reshape(v.shape[:-1] + (-1, 32))
    amax = np.abs(blocks).max(-1, keepdims=True)
    byte = np.maximum(np.where(amax > 0, np.frexp(amax)[1] - 1 + 127, 0) - down, 1)
    scale = np.exp2(byte - 127.0)
    codes = (blocks / scale).astype(np.float32).astype(dtype).astype(np.float64)
    return np.moveaxis((codes * scale).reshape(v.shape), -1, axis)


WIDE = False


def mx_kscale(k):
    if not WIDE:
        return np.ones(k)
    levels = np.array([10, -10, 5, -5, 0])
    a = np.random.permutation(np.resize(levels, k // 512 * 4)).reshape(k // 512, 4)
    idx = np.arange(k)
    return np.exp2(a[idx // 512, idx % 128 // 32])


BF16 = ml_dtypes.bfloat16


def bf(x):
    return np.asarray(x, np.float32).astype(BF16)


def f64(x):
    return np.asarray(x).astype(np.float64)


B, N, C, R, CO, L = 8, 512, 512, 128, 512, 2
C3 = 3 * C
EPS = 1e-5
LOGIT_STD = 2.5
X_STD = 1.5


def setup_inputs():
    t = mx_kscale(C3)
    th, tx = t[:C], t[C:C + C]
    tw = np.concatenate([th, tx, tx])
    e = np.exp(np.maximum(np.random.standard_normal((N, N)) * LOGIT_STD, 0.0))
    return {"h": bf(np.random.standard_normal((B, C, N)) * X_STD * th[None, :, None]),
            "x1": bf(np.random.standard_normal((B, C, N)) * 0.4 * tx[None, :, None]),
            "adp": bf(e / e.sum(1, keepdims=True)),
            "wg": bf(np.random.standard_normal((C, C3)) / np.sqrt(C) / tw[None, :]),
            "bg": bf(np.random.standard_normal(C) * 0.2),
            "gamma": bf(1.0 + 0.1 * np.random.standard_normal(C)),
            "beta": bf(np.random.standard_normal(C) * 0.2),
            "rmean": bf(np.random.standard_normal(C) * 0.2),
            "rvar": bf(np.random.uniform(0.5, 1.5, C))}


def reference(h, x1, adp, wg, bg, gamma, beta, rmean, rvar):
    h, x1 = f64(h), f64(x1)
    x2 = (mxq(x1.reshape(B * C, N), 1, "e4m3") @ mxq(f64(adp), 1, "e4m3").T).reshape(B, C, N)
    cat = np.concatenate([h, x1, x2], axis=1)
    g = (mxq(f64(wg), 1, "e4m3") @ mxq(cat, 1, "e4m3")) + f64(bg)[None, :, None]
    inv = f64(gamma) / np.sqrt(f64(rvar) + EPS)
    return g * inv[None, :, None] + (f64(beta) - f64(rmean) * inv)[None, :, None]

@@ -1,0 +1,236 @@
+from contextlib import ExitStack
+
+import concourse.mybir as mybir
+from concourse.masks import make_identity
+
+BF16 = mybir.dt.bfloat16
+F32 = mybir.dt.float32
+U32 = mybir.dt.uint32
+U8 = mybir.dt.uint8
+FP8X4 = mybir.dt.float8_e4m3fn_x4
+ACT = mybir.ActivationFunctionType
+ALU = mybir.AluOpType
+
+P = 128
+PACK = 4
+
+B = 8
+C = 512
+N = 512
+CO = 512
+STACKS = 3
+ROW_TILES = 4
+PSUM_BANKS = 8
+EPS = 1e-5
+VECTOR_BANK = 2
+
+FLOPS = 2 * B * C * N * N + 2 * B * CO * STACKS * C * N
+
+
+def half_of_the_words(words, u):
+    return words[:, u * P : (u + 1) * P]
+
+
+def every_second_word(words, u):
+    return words[:, u : 2 * P : 2]
+
+
+def tile_spatialgcn_pb_t_kernel(tc, h, x1, adp, wg, bg, gamma, beta, rmean, rvar, out):
+    nc = tc.nc
+    with ExitStack() as ctx:
+        ctx.enter_context(tc.manual_schedule())
+        const = ctx.enter_context(tc.tile_pool(name="const", bufs=1))
+        resident = ctx.enter_context(tc.tile_pool(name="resident", bufs=1))
+        work = ctx.enter_context(tc.tile_pool(name="work", bufs=3))
+        psum = ctx.enter_context(tc.psum_pool(name="psum", bufs=PSUM_BANKS))
+
+        per_channel = const.tile([P, 5, 16], BF16)
+        for i, vector in enumerate((rvar, gamma, bg, rmean, beta)):
+            nc.scalar.dma_start(
+                out=per_channel[:, i, 0:ROW_TILES], in_=vector.rearrange("(m r) -> m r", r=ROW_TILES)
+            )
+        rvar_sb, gamma_sb, bg_sb, rmean_sb, beta_sb = [per_channel[:, i, 0:ROW_TILES] for i in range(5)]
+
+        adp_sb = resident.tile([P, ROW_TILES * N], BF16)
+        nc.sync.dma_start(
+            out=adp_sb[:].rearrange("p (r v) -> p r v", r=ROW_TILES),
+            in_=adp.rearrange("(r p) v -> p r v", p=P),
+        )
+        x1_sb = [resident.tile([P, PACK * N], BF16, name="x1_sb%d" % b) for b in range(B)]
+        h_sb = [resident.tile([P, PACK * N], BF16, name="h_sb%d" % b) for b in range(B)]
+        wg_sb = [resident.tile([P, ROW_TILES * C], BF16, name="wg_sb%d" % s) for s in range(STACKS)]
+
+        def load_channels(dst, src):
+            nc.sync.dma_start(out=dst[:], in_=src.rearrange("(p j) n -> p (j n)", j=PACK))
+
+        load_channels(x1_sb[0], x1[0])
+        for s in range(STACKS):
+            nc.sync.dma_start(
+                out=wg_sb[s][:].rearrange("m (r c) -> m r c", r=ROW_TILES),
+                in_=wg[:, s * C : (s + 1) * C].rearrange("(m r) c -> m r c", r=ROW_TILES),
+            )
+        for b in range(B):
+            load_channels(h_sb[b], h[b])
+            if b + 1 < B:
+                load_channels(x1_sb[b + 1], x1[b + 1])
+
+        identity = const.tile([P, P], F32)
+        make_identity(nc, identity[:])
+
+        eps_column = const.tile([P, 1], F32)
+        nc.vector.memset(eps_column[:], EPS)
+        std = const.tile([P, ROW_TILES], F32)
+        nc.scalar.activation(out=std[:], in_=rvar_sb, func=ACT.Sqrt, bias=eps_column[:], scale=1.0)
+        inv = const.tile([P, ROW_TILES], F32)
+        nc.vector.reciprocal(out=inv[:], in_=std[:])
+        nc.vector.tensor_mul(out=inv[:], in0=inv[:], in1=gamma_sb)
+        shift = const.tile([P, ROW_TILES], F32)
+        nc.vector.tensor_sub(out=shift[:], in0=bg_sb, in1=rmean_sb)
+        nc.vector.tensor_mul(out=shift[:], in0=shift[:], in1=inv[:])
+        nc.vector.tensor_add(out=shift[:], in0=shift[:], in1=beta_sb)
+
+        def quantise(codes, scales, grouped):
+            nc.vector.quantize_mx(out=codes.bitcast(FP8X4), scales=scales, in_=grouped)
+
+        def flip(rows_sb, pick):
+            words = rows_sb[:].bitcast(F32).rearrange("p (r w) -> p r w", r=ROW_TILES)
+            grouped = work.tile([P, ROW_TILES * P * PACK], BF16, align_bytes=64, name="flipped")
+            grouped_words = grouped[:].bitcast(F32).rearrange("q (r m u) -> q r m u", r=ROW_TILES, u=2)
+            for pair in range(ROW_TILES // 2):
+                bank = psum.tile([P, 2, 2, P], F32, name="bank")
+                for r in range(2):
+                    for u in range(2):
+                        nc.tensor.transpose(bank[:, r, u, :], pick(words[:, 2 * pair + r, :], u), identity[:])
+                nc.scalar.copy(
+                    out=grouped_words[:, 2 * pair : 2 * pair + 2, :, :],
+                    in_=bank[:].rearrange("q r u m -> q r m u"),
+                )
+            return grouped
+
+        def regroup(dst, src):
+            nc.vector.tensor_copy(
+                out=dst.rearrange("p (c i j) -> p c j i", i=4, j=PACK),
+                in_=src.rearrange("p (j c i) -> p c j i", j=PACK, i=4),
+            )
+
+        adp_codes = const.tile([P, N], U32, align_bytes=64)
+        adp_scales = const.tile([P, N], U8, align_bytes=64)
+        wg_codes = const.tile([P, STACKS * CO], U32, align_bytes=64)
+        wg_scales = const.tile([P, STACKS * CO], U8, align_bytes=64)
+        wg_grouped, x1T_grouped, x1T_codes, x1T_scales = {}, {}, {}, {}
+        hx_grouped, x2_grouped, cat_codes, cat_scales, out_sb = {}, {}, {}, {}, {}
+
+        def flip_wg(s):
+            wg_grouped[s] = flip(wg_sb[s], every_second_word)
+
+        def quantise_wg(s):
+            quantise(wg_codes[:, s * CO : (s + 1) * CO], wg_scales[:, s * CO : (s + 1) * CO], wg_grouped[s][:])
+
+        def flip_x1(b):
+            x1T_grouped[b] = flip(x1_sb[b], half_of_the_words)
+
+        def quantise_x1T(b):
+            x1T_codes[b] = work.tile([P, C], U32, align_bytes=64, name="x1T_codes")
+            x1T_scales[b] = work.tile([P, C], U8, align_bytes=64, name="x1T_scales")
+            quantise(x1T_codes[b][:], x1T_scales[b][:], x1T_grouped[b][:])
+
+        def regroup_x1(b):
+            hx_grouped[b] = work.tile([P, 2 * N * PACK], BF16, align_bytes=64, name="hx_grouped")
+            regroup(hx_grouped[b][:, N * PACK : 2 * N * PACK], x1_sb[b][:])
+
+        def regroup_h(b):
+            regroup(hx_grouped[b][:, 0 : N * PACK], h_sb[b][:])
+
+        def quantise_h_and_x1(b):
+            cat_codes[b] = work.tile([P, STACKS * N], U32, align_bytes=64, name="cat_codes")
+            cat_scales[b] = work.tile([P, STACKS * N], U8, align_bytes=64, name="cat_scales")
+            quantise(cat_codes[b][:, 0 : 2 * N], cat_scales[b][:, 0 : 2 * N], hx_grouped[b][:])
+
+        def hop(b):
+            x2_grouped[b] = work.tile([P, N * PACK], BF16, align_bytes=64, name="x2_grouped")
+            for wc in range(N // P):
+                bank = psum.tile([P, PACK, P], F32, name="bank")
+                for j in range(PACK):
+                    nc.tensor.matmul_mx(
+                        out=bank[:, j, :],
+                        lhsT=x1T_codes[b][:, j * P : (j + 1) * P].bitcast(FP8X4),
+                        lhsT_scale=x1T_scales[b][:, j * P : (j + 1) * P],
+                        rhs=adp_codes[:, wc * P : (wc + 1) * P].bitcast(FP8X4),
+                        rhs_scale=adp_scales[:, wc * P : (wc + 1) * P],
+                        start=True,
+                        stop=True,
+                    )
+                nc.scalar.copy(
+                    out=x2_grouped[b][:, wc * P * PACK : (wc + 1) * P * PACK].rearrange("p (w j) -> p w j", j=PACK),
+                    in_=bank[:].rearrange("p j w -> p w j"),
+                )
+
+        def quantise_x2(b):
+            quantise(cat_codes[b][:, 2 * N : 3 * N], cat_scales[b][:, 2 * N : 3 * N], x2_grouped[b][:])
+
+        def conv(b):
+            out_sb[b] = work.tile([P, ROW_TILES * N], F32, name="out_sb")
+            for r in range(ROW_TILES):
+                bank = psum.tile([P, N], F32, name="bank")
+                for s in range(STACKS):
+                    nc.tensor.matmul_mx(
+                        out=bank[:],
+                        lhsT=wg_codes[:, s * CO + r * P : s * CO + (r + 1) * P].bitcast(FP8X4),
+                        lhsT_scale=wg_scales[:, s * CO + r * P : s * CO + (r + 1) * P],
+                        rhs=cat_codes[b][:, s * N : (s + 1) * N].bitcast(FP8X4),
+                        rhs_scale=cat_scales[b][:, s * N : (s + 1) * N],
+                        start=(s == 0),
+                        stop=(s == STACKS - 1),
+                    )
+                if r == VECTOR_BANK:
+                    nc.vector.tensor_scalar(
+                        out=out_sb[b][:, r * N : (r + 1) * N],
+                        in0=bank[:],
+                        scalar1=inv[:, r : r + 1],
+                        scalar2=shift[:, r : r + 1],
+                        op0=ALU.mult,
+                        op1=ALU.add,
+                    )
+                else:
+                    nc.scalar.activation(
+                        out=out_sb[b][:, r * N : (r + 1) * N],
+                        in_=bank[:],
+                        func=ACT.Identity,
+                        bias=shift[:, r : r + 1],
+                        scale=inv[:, r : r + 1],
+                    )
+                nc.sync.dma_start(
+                    out=out[b].rearrange("(m r) n -> m r n", r=ROW_TILES)[:, r, :],
+                    in_=out_sb[b][:, r * N : (r + 1) * N],
+                )
+
+        adp_grouped = flip(adp_sb, half_of_the_words)
+        flip_x1(0)
+        flip_wg(0)
+        flip_wg(1)
+        quantise(adp_codes[:], adp_scales[:], adp_grouped[:])
+        quantise_x1T(0)
+        regroup_x1(0)
+        hop(0)
+        quantise_wg(0)
+        quantise_wg(1)
+        regroup_h(0)
+        flip_wg(2)
+        quantise_h_and_x1(0)
+        quantise_x2(0)
+        quantise_wg(2)
+        flip_x1(1)
+        quantise_x1T(1)
+
+        for b in range(B):
+            if b + 1 < B:
+                regroup_x1(b + 1)
+                regroup_h(b + 1)
+            if b + 2 < B:
+                flip_x1(b + 2)
+                quantise_x1T(b + 2)
+            if b + 1 < B:
+                quantise_h_and_x1(b + 1)
+                hop(b + 1)
+                quantise_x2(b + 1)
+            conv(b)

@@ -9,7 +9,6 @@ U32 = mybir.dt.uint32
 U8 = mybir.dt.uint8
 FP8X4 = mybir.dt.float8_e4m3fn_x4
 ACT = mybir.ActivationFunctionType
-ALU = mybir.AluOpType
 
 P = 128
 PACK = 4
@@ -22,7 +21,6 @@ STACKS = 3
 ROW_TILES = 4
 PSUM_BANKS = 8
 EPS = 1e-5
-VECTOR_BANK = 2
 
 FLOPS = 2 * B * C * N * N + 2 * B * CO * STACKS * C * N
 
@@ -182,23 +180,13 @@ def tile_spatialgcn_pb_t_kernel(tc, h, x1, adp, wg, bg, gamma, beta, rmean, rvar
                         start=(s == 0),
                         stop=(s == STACKS - 1),
                     )
-                if r == VECTOR_BANK:
-                    nc.vector.tensor_scalar(
-                        out=out_sb[b][:, r * N : (r + 1) * N],
-                        in0=bank[:],
-                        scalar1=inv[:, r : r + 1],
-                        scalar2=shift[:, r : r + 1],
-                        op0=ALU.mult,
-                        op1=ALU.add,
-                    )
-                else:
-                    nc.scalar.activation(
-                        out=out_sb[b][:, r * N : (r + 1) * N],
-                        in_=bank[:],
-                        func=ACT.Identity,
-                        bias=shift[:, r : r + 1],
-                        scale=inv[:, r : r + 1],
-                    )
+                nc.scalar.activation(
+                    out=out_sb[b][:, r * N : (r + 1) * N],
+                    in_=bank[:],
+                    func=ACT.Identity,
+                    bias=shift[:, r : r + 1],
+                    scale=inv[:, r : r + 1],
+                )
                 nc.sync.dma_start(
                     out=out[b].rearrange("(m r) n -> m r n", r=ROW_TILES)[:, r, :],
                     in_=out_sb[b][:, r * N : (r + 1) * N],

@@ -25,14 +25,6 @@ EPS = 1e-5
 FLOPS = 2 * B * C * N * N + 2 * B * CO * STACKS * C * N
 
 
-def half_of_the_words(words, u):
-    return words[:, u * P : (u + 1) * P]
-
-
-def every_second_word(words, u):
-    return words[:, u : 2 * P : 2]
-
-
 def tile_spatialgcn_pb_t_kernel(tc, h, x1, adp, wg, bg, gamma, beta, rmean, rvar, out):
     nc = tc.nc
     with ExitStack() as ctx:
@@ -59,7 +51,9 @@ def tile_spatialgcn_pb_t_kernel(tc, h, x1, adp, wg, bg, gamma, beta, rmean, rvar
         wg_sb = [resident.tile([P, ROW_TILES * C], BF16, name="wg_sb%d" % s) for s in range(STACKS)]
 
         def load_channels(dst, src):
-            nc.sync.dma_start(out=dst[:], in_=src.rearrange("(p j) n -> p (j n)", j=PACK))
+            nc.sync.dma_start(
+                out=dst[:].rearrange("p (u f) -> p u f", u=2), in_=src.rearrange("(u p e) n -> p u (e n)", u=2, e=2)
+            )
 
         load_channels(x1_sb[0], x1[0])
         for s in range(STACKS):
@@ -90,7 +84,7 @@ def tile_spatialgcn_pb_t_kernel(tc, h, x1, adp, wg, bg, gamma, beta, rmean, rvar
         def quantise(codes, scales, grouped):
             nc.vector.quantize_mx(out=codes.bitcast(FP8X4), scales=scales, in_=grouped)
 
-        def flip(rows_sb, pick):
+        def flip(rows_sb):
             words = rows_sb[:].bitcast(F32).rearrange("p (r w) -> p r w", r=ROW_TILES)
             grouped = work.tile([P, ROW_TILES * P * PACK], BF16, align_bytes=64, name="flipped")
             grouped_words = grouped[:].bitcast(F32).rearrange("q (r m u) -> q r m u", r=ROW_TILES, u=2)
@@ -98,7 +92,7 @@ def tile_spatialgcn_pb_t_kernel(tc, h, x1, adp, wg, bg, gamma, beta, rmean, rvar
                 bank = psum.tile([P, 2, 2, P], F32, name="bank")
                 for r in range(2):
                     for u in range(2):
-                        nc.tensor.transpose(bank[:, r, u, :], pick(words[:, 2 * pair + r, :], u), identity[:])
+                        nc.tensor.transpose(bank[:, r, u, :], words[:, 2 * pair + r, u * P : (u + 1) * P], identity[:])
                 nc.scalar.copy(
                     out=grouped_words[:, 2 * pair : 2 * pair + 2, :, :],
                     in_=bank[:].rearrange("q r u m -> q r m u"),
@@ -119,13 +113,13 @@ def tile_spatialgcn_pb_t_kernel(tc, h, x1, adp, wg, bg, gamma, beta, rmean, rvar
         hx_grouped, x2_grouped, cat_codes, cat_scales, out_sb = {}, {}, {}, {}, {}
 
         def flip_wg(s):
-            wg_grouped[s] = flip(wg_sb[s], every_second_word)
+            wg_grouped[s] = flip(wg_sb[s])
 
         def quantise_wg(s):
             quantise(wg_codes[:, s * CO : (s + 1) * CO], wg_scales[:, s * CO : (s + 1) * CO], wg_grouped[s][:])
 
         def flip_x1(b):
-            x1T_grouped[b] = flip(x1_sb[b], half_of_the_words)
+            x1T_grouped[b] = flip(x1_sb[b])
 
         def quantise_x1T(b):
             x1T_codes[b] = work.tile([P, C], U32, align_bytes=64, name="x1T_codes")
@@ -192,7 +186,7 @@ def tile_spatialgcn_pb_t_kernel(tc, h, x1, adp, wg, bg, gamma, beta, rmean, rvar
                     in_=out_sb[b][:, r * N : (r + 1) * N],
                 )
 
-        adp_grouped = flip(adp_sb, half_of_the_words)
+        adp_grouped = flip(adp_sb)
         flip_x1(0)
         flip_wg(0)
         flip_wg(1)

@@ -9,6 +9,7 @@ U32 = mybir.dt.uint32
 U8 = mybir.dt.uint8
 FP8X4 = mybir.dt.float8_e4m3fn_x4
 ACT = mybir.ActivationFunctionType
+ALU = mybir.AluOpType
 
 P = 128
 PACK = 4
@@ -42,10 +43,6 @@ def tile_spatialgcn_pb_t_kernel(tc, h, x1, adp, wg, bg, gamma, beta, rmean, rvar
         rvar_sb, gamma_sb, bg_sb, rmean_sb, beta_sb = [per_channel[:, i, 0:ROW_TILES] for i in range(5)]
 
         adp_sb = resident.tile([P, ROW_TILES * N], BF16)
-        nc.sync.dma_start(
-            out=adp_sb[:].rearrange("p (r v) -> p r v", r=ROW_TILES),
-            in_=adp.rearrange("(r p) v -> p r v", p=P),
-        )
         x1_sb = [resident.tile([P, PACK * N], BF16, name="x1_sb%d" % b) for b in range(B)]
         h_sb = [resident.tile([P, PACK * N], BF16, name="h_sb%d" % b) for b in range(B)]
         wg_sb = [resident.tile([P, ROW_TILES * C], BF16, name="wg_sb%d" % s) for s in range(STACKS)]
@@ -55,16 +52,28 @@ def tile_spatialgcn_pb_t_kernel(tc, h, x1, adp, wg, bg, gamma, beta, rmean, rvar
                 out=dst[:].rearrange("p (u f) -> p u f", u=2), in_=src.rearrange("(u p e) n -> p u (e n)", u=2, e=2)
             )
 
-        load_channels(x1_sb[0], x1[0])
-        for s in range(STACKS):
+        def load_wg(s):
             nc.sync.dma_start(
                 out=wg_sb[s][:].rearrange("m (r c) -> m r c", r=ROW_TILES),
                 in_=wg[:, s * C : (s + 1) * C].rearrange("(m r) c -> m r c", r=ROW_TILES),
             )
-        for b in range(B):
+
+        for u in range(2):
+            nc.sync.dma_start(
+                out=x1_sb[0][:, u * 2 * N : (u + 1) * 2 * N],
+                in_=x1[0][u * 2 * P : (u + 1) * 2 * P, :].rearrange("(p e) n -> p (e n)", e=2),
+            )
+        nc.sync.dma_start(
+            out=adp_sb[:].rearrange("p (r v) -> p r v", r=ROW_TILES),
+            in_=adp.rearrange("(r p) v -> p r v", p=P),
+        )
+        load_wg(1)
+        load_wg(0)
+        load_channels(h_sb[0], h[0])
+        load_wg(2)
+        for b in range(1, B):
+            load_channels(x1_sb[b], x1[b])
             load_channels(h_sb[b], h[b])
-            if b + 1 < B:
-                load_channels(x1_sb[b + 1], x1[b + 1])
 
         identity = const.tile([P, P], F32)
         make_identity(nc, identity[:])
@@ -84,18 +93,25 @@ def tile_spatialgcn_pb_t_kernel(tc, h, x1, adp, wg, bg, gamma, beta, rmean, rvar
         def quantise(codes, scales, grouped):
             nc.vector.quantize_mx(out=codes.bitcast(FP8X4), scales=scales, in_=grouped)
 
-        def flip(rows_sb):
+        def empty(engine, out, in_):
+            if engine == "V":
+                nc.vector.tensor_copy(out=out, in_=in_)
+            else:
+                nc.scalar.copy(out=out, in_=in_)
+
+        def flip(rows_sb, engines="SS"):
             words = rows_sb[:].bitcast(F32).rearrange("p (r w) -> p r w", r=ROW_TILES)
-            grouped = work.tile([P, ROW_TILES * P * PACK], BF16, align_bytes=64, name="flipped")
+            grouped = work.tile([P, ROW_TILES * P * PACK], BF16, align_bytes=64, name="flipped", bufs=4)
             grouped_words = grouped[:].bitcast(F32).rearrange("q (r m u) -> q r m u", r=ROW_TILES, u=2)
             for pair in range(ROW_TILES // 2):
                 bank = psum.tile([P, 2, 2, P], F32, name="bank")
                 for r in range(2):
                     for u in range(2):
                         nc.tensor.transpose(bank[:, r, u, :], words[:, 2 * pair + r, u * P : (u + 1) * P], identity[:])
-                nc.scalar.copy(
-                    out=grouped_words[:, 2 * pair : 2 * pair + 2, :, :],
-                    in_=bank[:].rearrange("q r u m -> q r m u"),
+                empty(
+                    engines[pair],
+                    grouped_words[:, 2 * pair : 2 * pair + 2, :, :],
+                    bank[:].rearrange("q r u m -> q r m u"),
                 )
             return grouped
 
@@ -112,8 +128,8 @@ def tile_spatialgcn_pb_t_kernel(tc, h, x1, adp, wg, bg, gamma, beta, rmean, rvar
         wg_grouped, x1T_grouped, x1T_codes, x1T_scales = {}, {}, {}, {}
         hx_grouped, x2_grouped, cat_codes, cat_scales, out_sb = {}, {}, {}, {}, {}
 
-        def flip_wg(s):
-            wg_grouped[s] = flip(wg_sb[s])
+        def flip_wg(s, engines="SS"):
+            wg_grouped[s] = flip(wg_sb[s], engines)
 
         def quantise_wg(s):
             quantise(wg_codes[:, s * CO : (s + 1) * CO], wg_scales[:, s * CO : (s + 1) * CO], wg_grouped[s][:])
@@ -126,19 +142,25 @@ def tile_spatialgcn_pb_t_kernel(tc, h, x1, adp, wg, bg, gamma, beta, rmean, rvar
             x1T_scales[b] = work.tile([P, C], U8, align_bytes=64, name="x1T_scales")
             quantise(x1T_codes[b][:], x1T_scales[b][:], x1T_grouped[b][:])
 
-        def regroup_x1(b):
+        def open_batch(b):
             hx_grouped[b] = work.tile([P, 2 * N * PACK], BF16, align_bytes=64, name="hx_grouped")
+            cat_codes[b] = work.tile([P, STACKS * N], U32, align_bytes=64, name="cat_codes")
+            cat_scales[b] = work.tile([P, STACKS * N], U8, align_bytes=64, name="cat_scales")
+
+        def regroup_x1(b):
             regroup(hx_grouped[b][:, N * PACK : 2 * N * PACK], x1_sb[b][:])
 
         def regroup_h(b):
             regroup(hx_grouped[b][:, 0 : N * PACK], h_sb[b][:])
 
-        def quantise_h_and_x1(b):
-            cat_codes[b] = work.tile([P, STACKS * N], U32, align_bytes=64, name="cat_codes")
-            cat_scales[b] = work.tile([P, STACKS * N], U8, align_bytes=64, name="cat_scales")
-            quantise(cat_codes[b][:, 0 : 2 * N], cat_scales[b][:, 0 : 2 * N], hx_grouped[b][:])
+        def quantise_stacks(b, first, last):
+            quantise(
+                cat_codes[b][:, first * N : (last + 1) * N],
+                cat_scales[b][:, first * N : (last + 1) * N],
+                hx_grouped[b][:, first * N * PACK : (last + 1) * N * PACK],
+            )
 
-        def hop(b):
+        def hop(b, engines="SSSS"):
             x2_grouped[b] = work.tile([P, N * PACK], BF16, align_bytes=64, name="x2_grouped")
             for wc in range(N // P):
                 bank = psum.tile([P, PACK, P], F32, name="bank")
@@ -152,67 +174,106 @@ def tile_spatialgcn_pb_t_kernel(tc, h, x1, adp, wg, bg, gamma, beta, rmean, rvar
                         start=True,
                         stop=True,
                     )
-                nc.scalar.copy(
-                    out=x2_grouped[b][:, wc * P * PACK : (wc + 1) * P * PACK].rearrange("p (w j) -> p w j", j=PACK),
-                    in_=bank[:].rearrange("p j w -> p w j"),
+                empty(
+                    engines[wc],
+                    x2_grouped[b][:, wc * P * PACK : (wc + 1) * P * PACK].rearrange("p (w j) -> p w j", j=PACK),
+                    bank[:].rearrange("p j w -> p w j"),
                 )
 
         def quantise_x2(b):
             quantise(cat_codes[b][:, 2 * N : 3 * N], cat_scales[b][:, 2 * N : 3 * N], x2_grouped[b][:])
 
-        def conv(b):
+        def conv_pass(b, bank, r, s, start, stop):
+            nc.tensor.matmul_mx(
+                out=bank[:],
+                lhsT=wg_codes[:, s * CO + r * P : s * CO + (r + 1) * P].bitcast(FP8X4),
+                lhsT_scale=wg_scales[:, s * CO + r * P : s * CO + (r + 1) * P],
+                rhs=cat_codes[b][:, s * N : (s + 1) * N].bitcast(FP8X4),
+                rhs_scale=cat_scales[b][:, s * N : (s + 1) * N],
+                start=start,
+                stop=stop,
+            )
+
+        def finish(b, bank, r, engine):
+            rows = out_sb[b][:, r * N : (r + 1) * N]
+            if engine == "V":
+                nc.vector.tensor_scalar(
+                    out=rows, in0=bank[:], scalar1=inv[:, r : r + 1], scalar2=shift[:, r : r + 1], op0=ALU.mult, op1=ALU.add
+                )
+            else:
+                nc.scalar.activation(
+                    out=rows, in_=bank[:], func=ACT.Identity, bias=shift[:, r : r + 1], scale=inv[:, r : r + 1]
+                )
+            nc.sync.dma_start(out=out[b].rearrange("(m r) n -> m r n", r=ROW_TILES)[:, r, :], in_=rows)
+
+        def conv(b, engines="SSSS"):
             out_sb[b] = work.tile([P, ROW_TILES * N], F32, name="out_sb")
             for r in range(ROW_TILES):
                 bank = psum.tile([P, N], F32, name="bank")
                 for s in range(STACKS):
-                    nc.tensor.matmul_mx(
-                        out=bank[:],
-                        lhsT=wg_codes[:, s * CO + r * P : s * CO + (r + 1) * P].bitcast(FP8X4),
-                        lhsT_scale=wg_scales[:, s * CO + r * P : s * CO + (r + 1) * P],
-                        rhs=cat_codes[b][:, s * N : (s + 1) * N].bitcast(FP8X4),
-                        rhs_scale=cat_scales[b][:, s * N : (s + 1) * N],
-                        start=(s == 0),
-                        stop=(s == STACKS - 1),
-                    )
-                nc.scalar.activation(
-                    out=out_sb[b][:, r * N : (r + 1) * N],
-                    in_=bank[:],
-                    func=ACT.Identity,
-                    bias=shift[:, r : r + 1],
-                    scale=inv[:, r : r + 1],
-                )
-                nc.sync.dma_start(
-                    out=out[b].rearrange("(m r) n -> m r n", r=ROW_TILES)[:, r, :],
-                    in_=out_sb[b][:, r * N : (r + 1) * N],
-                )
+                    conv_pass(b, bank, r, s, s == 0, s == STACKS - 1)
+                finish(b, bank, r, engines[r])
 
-        adp_grouped = flip(adp_sb)
+        def conv_x2_last(b, engines):
+            out_sb[b] = work.tile([P, ROW_TILES * N], F32, name="out_sb")
+            banks = {}
+            for r in range(ROW_TILES):
+                banks[r] = psum.tile([P, N], F32, name="bank")
+                conv_pass(b, banks[r], r, 1, True, False)
+                conv_pass(b, banks[r], r, 0, False, False)
+            for r in range(ROW_TILES):
+                conv_pass(b, banks[r], r, 2, False, True)
+                finish(b, banks[r], r, engines[r])
+
+        open_batch(0)
         flip_x1(0)
-        flip_wg(0)
+        regroup_x1(0)
+        adp_grouped = flip(adp_sb)
+        quantise_x1T(0)
         flip_wg(1)
         quantise(adp_codes[:], adp_scales[:], adp_grouped[:])
-        quantise_x1T(0)
-        regroup_x1(0)
-        hop(0)
-        quantise_wg(0)
+        quantise_stacks(0, 1, 1)
+        flip_wg(0)
         quantise_wg(1)
+        hop(0)
         regroup_h(0)
-        flip_wg(2)
-        quantise_h_and_x1(0)
-        quantise_x2(0)
+        quantise_wg(0)
+        quantise_stacks(0, 0, 0)
+        flip_wg(2, "VS")
         quantise_wg(2)
         flip_x1(1)
+        quantise_x2(0)
         quantise_x1T(1)
+        open_batch(1)
+        regroup_h(1)
+        regroup_x1(1)
+        conv_x2_last(0, "SSSV")
+        flip_x1(2)
+        quantise_stacks(1, 0, 0)
+        quantise_x1T(2)
+        hop(1, "SSVS")
+        quantise_stacks(1, 1, 1)
+        flip_x1(3)
+        quantise_x2(1)
+        hop(2)
+        open_batch(2)
+        regroup_x1(2)
+        regroup_h(2)
+        quantise_x1T(3)
+        quantise_stacks(2, 0, 1)
+        quantise_x2(2)
+        conv(1)
 
-        for b in range(B):
+        for b in range(2, B):
             if b + 1 < B:
+                open_batch(b + 1)
                 regroup_x1(b + 1)
                 regroup_h(b + 1)
             if b + 2 < B:
                 flip_x1(b + 2)
                 quantise_x1T(b + 2)
             if b + 1 < B:
-                quantise_h_and_x1(b + 1)
+                quantise_stacks(b + 1, 0, 1)
                 hop(b + 1)
                 quantise_x2(b + 1)
-            conv(b)
+            conv(b, "SSSS" if b + 1 < B else "VSVS")

@@ -269,8 +269,10 @@ def tile_spatialgcn_pb_t_kernel(tc, h, x1, adp, wg, bg, gamma, beta, rmean, rvar
                 open_batch(b + 1)
                 regroup_x1(b + 1)
                 regroup_h(b + 1)
+            if b % 2 == 0:
+                for later in range(b + 2, min(b + 4, B)):
+                    flip_x1(later)
             if b + 2 < B:
-                flip_x1(b + 2)
                 quantise_x1T(b + 2)
             if b + 1 < B:
                 quantise_stacks(b + 1, 0, 1)

@@ -183,47 +183,59 @@ def tile_spatialgcn_pb_t_kernel(tc, h, x1, adp, wg, bg, gamma, beta, rmean, rvar
         def quantise_x2(b):
             quantise(cat_codes[b][:, 2 * N : 3 * N], cat_scales[b][:, 2 * N : 3 * N], x2_grouped[b][:])
 
-        def conv_pass(b, bank, r, s, start, stop):
+        def conv_pass(b, out_, r, s, start, stop, first=0, width=N):
+            columns = slice(s * N + first, s * N + first + width)
             nc.tensor.matmul_mx(
-                out=bank[:],
+                out=out_,
                 lhsT=wg_codes[:, s * CO + r * P : s * CO + (r + 1) * P].bitcast(FP8X4),
                 lhsT_scale=wg_scales[:, s * CO + r * P : s * CO + (r + 1) * P],
-                rhs=cat_codes[b][:, s * N : (s + 1) * N].bitcast(FP8X4),
-                rhs_scale=cat_scales[b][:, s * N : (s + 1) * N],
+                rhs=cat_codes[b][:, columns].bitcast(FP8X4),
+                rhs_scale=cat_scales[b][:, columns],
                 start=start,
                 stop=stop,
             )
 
-        def finish(b, bank, r, engine):
-            rows = out_sb[b][:, r * N : (r + 1) * N]
+        def finish(b, in_, r, engine, first=0, width=N):
+            rows = out_sb[b][:, r * N + first : r * N + first + width]
             if engine == "V":
                 nc.vector.tensor_scalar(
-                    out=rows, in0=bank[:], scalar1=inv[:, r : r + 1], scalar2=shift[:, r : r + 1], op0=ALU.mult, op1=ALU.add
+                    out=rows, in0=in_, scalar1=inv[:, r : r + 1], scalar2=shift[:, r : r + 1], op0=ALU.mult, op1=ALU.add
                 )
             else:
                 nc.scalar.activation(
-                    out=rows, in_=bank[:], func=ACT.Identity, bias=shift[:, r : r + 1], scale=inv[:, r : r + 1]
+                    out=rows, in_=in_, func=ACT.Identity, bias=shift[:, r : r + 1], scale=inv[:, r : r + 1]
                 )
-            nc.sync.dma_start(out=out[b].rearrange("(m r) n -> m r n", r=ROW_TILES)[:, r, :], in_=rows)
+            nc.sync.dma_start(
+                out=out[b].rearrange("(m r) n -> m r n", r=ROW_TILES)[:, r, first : first + width], in_=rows
+            )
 
         def conv(b, engines="SSSS"):
             out_sb[b] = work.tile([P, ROW_TILES * N], F32, name="out_sb")
-            for r in range(ROW_TILES):
+            for r in range(len(engines)):
                 bank = psum.tile([P, N], F32, name="bank")
                 for s in range(STACKS):
-                    conv_pass(b, bank, r, s, s == 0, s == STACKS - 1)
-                finish(b, bank, r, engines[r])
+                    conv_pass(b, bank[:], r, s, s == 0, s == STACKS - 1)
+                finish(b, bank[:], r, engines[r])
+
+        def conv_last_rows(b):
+            r = ROW_TILES - 1
+            half = N // 2
+            for first, engine in ((0, "V"), (half, "S")):
+                bank = psum.tile([P, N], F32, name="bank")
+                for s in range(STACKS):
+                    conv_pass(b, bank[:, 0:half], r, s, s == 0, s == STACKS - 1, first, half)
+                finish(b, bank[:, 0:half], r, engine, first, half)
 
         def conv_x2_last(b, engines):
             out_sb[b] = work.tile([P, ROW_TILES * N], F32, name="out_sb")
             banks = {}
             for r in range(ROW_TILES):
                 banks[r] = psum.tile([P, N], F32, name="bank")
-                conv_pass(b, banks[r], r, 1, True, False)
-                conv_pass(b, banks[r], r, 0, False, False)
+                conv_pass(b, banks[r][:], r, 1, True, False)
+                conv_pass(b, banks[r][:], r, 0, False, False)
             for r in range(ROW_TILES):
-                conv_pass(b, banks[r], r, 2, False, True)
-                finish(b, banks[r], r, engines[r])
+                conv_pass(b, banks[r][:], r, 2, False, True)
+                finish(b, banks[r][:], r, engines[r])
 
         open_batch(0)
         flip_x1(0)
@@ -278,4 +290,5 @@ def tile_spatialgcn_pb_t_kernel(tc, h, x1, adp, wg, bg, gamma, beta, rmean, rvar
                 quantise_stacks(b + 1, 0, 1)
                 hop(b + 1)
                 quantise_x2(b + 1)
-            conv(b, "SSSS" if b + 1 < B else "VSVS")
+            conv(b, "SSSS" if b + 1 < B else "SVS")
+        conv_last_rows(B - 1)

from contextlib import ExitStack

import concourse.mybir as mybir
from concourse.masks import make_identity

BF16 = mybir.dt.bfloat16
F32 = mybir.dt.float32
U32 = mybir.dt.uint32
U8 = mybir.dt.uint8
FP8X4 = mybir.dt.float8_e4m3fn_x4
ACT = mybir.ActivationFunctionType
ALU = mybir.AluOpType

P = 128
PACK = 4

B = 8
C = 512
N = 512
CO = 512
STACKS = 3
ROW_TILES = 4
PSUM_BANKS = 8
EPS = 1e-5

FLOPS = 2 * B * C * N * N + 2 * B * CO * STACKS * C * N


def tile_spatialgcn_pb_t_kernel(tc, h, x1, adp, wg, bg, gamma, beta, rmean, rvar, out):
    nc = tc.nc
    with ExitStack() as ctx:
        ctx.enter_context(tc.manual_schedule())
        const = ctx.enter_context(tc.tile_pool(name="const", bufs=1))
        resident = ctx.enter_context(tc.tile_pool(name="resident", bufs=1))
        work = ctx.enter_context(tc.tile_pool(name="work", bufs=3))
        psum = ctx.enter_context(tc.psum_pool(name="psum", bufs=PSUM_BANKS))

        per_channel = const.tile([P, 5, 16], BF16)
        for i, vector in enumerate((rvar, gamma, bg, rmean, beta)):
            nc.scalar.dma_start(
                out=per_channel[:, i, 0:ROW_TILES], in_=vector.rearrange("(m r) -> m r", r=ROW_TILES)
            )
        rvar_sb, gamma_sb, bg_sb, rmean_sb, beta_sb = [per_channel[:, i, 0:ROW_TILES] for i in range(5)]

        adp_sb = resident.tile([P, ROW_TILES * N], BF16)
        x1_sb = [resident.tile([P, PACK * N], BF16, name="x1_sb%d" % b) for b in range(B)]
        h_sb = [resident.tile([P, PACK * N], BF16, name="h_sb%d" % b) for b in range(B)]
        wg_sb = [resident.tile([P, ROW_TILES * C], BF16, name="wg_sb%d" % s) for s in range(STACKS)]

        def load_channels(dst, src):
            nc.sync.dma_start(
                out=dst[:].rearrange("p (u f) -> p u f", u=2), in_=src.rearrange("(u p e) n -> p u (e n)", u=2, e=2)
            )

        def load_wg(s):
            nc.sync.dma_start(
                out=wg_sb[s][:].rearrange("m (r c) -> m r c", r=ROW_TILES),
                in_=wg[:, s * C : (s + 1) * C].rearrange("(m r) c -> m r c", r=ROW_TILES),
            )

        for u in range(2):
            nc.sync.dma_start(
                out=x1_sb[0][:, u * 2 * N : (u + 1) * 2 * N],
                in_=x1[0][u * 2 * P : (u + 1) * 2 * P, :].rearrange("(p e) n -> p (e n)", e=2),
            )
        nc.sync.dma_start(
            out=adp_sb[:].rearrange("p (r v) -> p r v", r=ROW_TILES),
            in_=adp.rearrange("(r p) v -> p r v", p=P),
        )
        load_wg(1)
        load_wg(0)
        load_channels(h_sb[0], h[0])
        load_wg(2)
        for b in range(1, B):
            load_channels(x1_sb[b], x1[b])
            load_channels(h_sb[b], h[b])

        identity = const.tile([P, P], F32)
        make_identity(nc, identity[:])

        eps_column = const.tile([P, 1], F32)
        nc.vector.memset(eps_column[:], EPS)
        std = const.tile([P, ROW_TILES], F32)
        nc.scalar.activation(out=std[:], in_=rvar_sb, func=ACT.Sqrt, bias=eps_column[:], scale=1.0)
        inv = const.tile([P, ROW_TILES], F32)
        nc.vector.reciprocal(out=inv[:], in_=std[:])
        nc.vector.tensor_mul(out=inv[:], in0=inv[:], in1=gamma_sb)
        shift = const.tile([P, ROW_TILES], F32)
        nc.vector.tensor_sub(out=shift[:], in0=bg_sb, in1=rmean_sb)
        nc.vector.tensor_mul(out=shift[:], in0=shift[:], in1=inv[:])
        nc.vector.tensor_add(out=shift[:], in0=shift[:], in1=beta_sb)

        def quantise(codes, scales, grouped):
            nc.vector.quantize_mx(out=codes.bitcast(FP8X4), scales=scales, in_=grouped)

        def empty(engine, out, in_):
            if engine == "V":
                nc.vector.tensor_copy(out=out, in_=in_)
            else:
                nc.scalar.copy(out=out, in_=in_)

        def flip(rows_sb, engines="SS"):
            words = rows_sb[:].bitcast(F32).rearrange("p (r w) -> p r w", r=ROW_TILES)
            grouped = work.tile([P, ROW_TILES * P * PACK], BF16, align_bytes=64, name="flipped", bufs=4)
            grouped_words = grouped[:].bitcast(F32).rearrange("q (r m u) -> q r m u", r=ROW_TILES, u=2)
            for pair in range(ROW_TILES // 2):
                bank = psum.tile([P, 2, 2, P], F32, name="bank")
                for r in range(2):
                    for u in range(2):
                        nc.tensor.transpose(bank[:, r, u, :], words[:, 2 * pair + r, u * P : (u + 1) * P], identity[:])
                empty(
                    engines[pair],
                    grouped_words[:, 2 * pair : 2 * pair + 2, :, :],
                    bank[:].rearrange("q r u m -> q r m u"),
                )
            return grouped

        def regroup(dst, src):
            nc.vector.tensor_copy(
                out=dst.rearrange("p (c i j) -> p c j i", i=4, j=PACK),
                in_=src.rearrange("p (j c i) -> p c j i", j=PACK, i=4),
            )

        adp_codes = const.tile([P, N], U32, align_bytes=64)
        adp_scales = const.tile([P, N], U8, align_bytes=64)
        wg_codes = const.tile([P, STACKS * CO], U32, align_bytes=64)
        wg_scales = const.tile([P, STACKS * CO], U8, align_bytes=64)
        wg_grouped, x1T_grouped, x1T_codes, x1T_scales = {}, {}, {}, {}
        hx_grouped, x2_grouped, cat_codes, cat_scales, out_sb = {}, {}, {}, {}, {}

        def flip_wg(s, engines="SS"):
            wg_grouped[s] = flip(wg_sb[s], engines)

        def quantise_wg(s):
            quantise(wg_codes[:, s * CO : (s + 1) * CO], wg_scales[:, s * CO : (s + 1) * CO], wg_grouped[s][:])

        def flip_x1(b):
            x1T_grouped[b] = flip(x1_sb[b])

        def quantise_x1T(b):
            x1T_codes[b] = work.tile([P, C], U32, align_bytes=64, name="x1T_codes")
            x1T_scales[b] = work.tile([P, C], U8, align_bytes=64, name="x1T_scales")
            quantise(x1T_codes[b][:], x1T_scales[b][:], x1T_grouped[b][:])

        def open_batch(b):
            hx_grouped[b] = work.tile([P, 2 * N * PACK], BF16, align_bytes=64, name="hx_grouped")
            cat_codes[b] = work.tile([P, STACKS * N], U32, align_bytes=64, name="cat_codes")
            cat_scales[b] = work.tile([P, STACKS * N], U8, align_bytes=64, name="cat_scales")

        def regroup_x1(b):
            regroup(hx_grouped[b][:, N * PACK : 2 * N * PACK], x1_sb[b][:])

        def regroup_h(b):
            regroup(hx_grouped[b][:, 0 : N * PACK], h_sb[b][:])

        def quantise_stacks(b, first, last):
            quantise(
                cat_codes[b][:, first * N : (last + 1) * N],
                cat_scales[b][:, first * N : (last + 1) * N],
                hx_grouped[b][:, first * N * PACK : (last + 1) * N * PACK],
            )

        def hop(b, engines="SSSS"):
            x2_grouped[b] = work.tile([P, N * PACK], BF16, align_bytes=64, name="x2_grouped")
            for wc in range(N // P):
                bank = psum.tile([P, PACK, P], F32, name="bank")
                for j in range(PACK):
                    nc.tensor.matmul_mx(
                        out=bank[:, j, :],
                        lhsT=x1T_codes[b][:, j * P : (j + 1) * P].bitcast(FP8X4),
                        lhsT_scale=x1T_scales[b][:, j * P : (j + 1) * P],
                        rhs=adp_codes[:, wc * P : (wc + 1) * P].bitcast(FP8X4),
                        rhs_scale=adp_scales[:, wc * P : (wc + 1) * P],
                        start=True,
                        stop=True,
                    )
                empty(
                    engines[wc],
                    x2_grouped[b][:, wc * P * PACK : (wc + 1) * P * PACK].rearrange("p (w j) -> p w j", j=PACK),
                    bank[:].rearrange("p j w -> p w j"),
                )

        def quantise_x2(b):
            quantise(cat_codes[b][:, 2 * N : 3 * N], cat_scales[b][:, 2 * N : 3 * N], x2_grouped[b][:])

        def conv_pass(b, out_, r, s, start, stop, first=0, width=N):
            columns = slice(s * N + first, s * N + first + width)
            nc.tensor.matmul_mx(
                out=out_,
                lhsT=wg_codes[:, s * CO + r * P : s * CO + (r + 1) * P].bitcast(FP8X4),
                lhsT_scale=wg_scales[:, s * CO + r * P : s * CO + (r + 1) * P],
                rhs=cat_codes[b][:, columns].bitcast(FP8X4),
                rhs_scale=cat_scales[b][:, columns],
                start=start,
                stop=stop,
            )

        def finish(b, in_, r, engine, first=0, width=N):
            rows = out_sb[b][:, r * N + first : r * N + first + width]
            if engine == "V":
                nc.vector.tensor_scalar(
                    out=rows, in0=in_, scalar1=inv[:, r : r + 1], scalar2=shift[:, r : r + 1], op0=ALU.mult, op1=ALU.add
                )
            else:
                nc.scalar.activation(
                    out=rows, in_=in_, func=ACT.Identity, bias=shift[:, r : r + 1], scale=inv[:, r : r + 1]
                )
            nc.sync.dma_start(
                out=out[b].rearrange("(m r) n -> m r n", r=ROW_TILES)[:, r, first : first + width], in_=rows
            )

        def conv(b, engines="SSSS"):
            out_sb[b] = work.tile([P, ROW_TILES * N], F32, name="out_sb")
            for r in range(len(engines)):
                bank = psum.tile([P, N], F32, name="bank")
                for s in range(STACKS):
                    conv_pass(b, bank[:], r, s, s == 0, s == STACKS - 1)
                finish(b, bank[:], r, engines[r])

        def conv_last_rows(b):
            r = ROW_TILES - 1
            half = N // 2
            for first, engine in ((0, "V"), (half, "S")):
                bank = psum.tile([P, N], F32, name="bank")
                for s in range(STACKS):
                    conv_pass(b, bank[:, 0:half], r, s, s == 0, s == STACKS - 1, first, half)
                finish(b, bank[:, 0:half], r, engine, first, half)

        def conv_x2_last(b, engines):
            out_sb[b] = work.tile([P, ROW_TILES * N], F32, name="out_sb")
            banks = {}
            for r in range(ROW_TILES):
                banks[r] = psum.tile([P, N], F32, name="bank")
                conv_pass(b, banks[r][:], r, 1, True, False)
                conv_pass(b, banks[r][:], r, 0, False, False)
            for r in range(ROW_TILES):
                conv_pass(b, banks[r][:], r, 2, False, True)
                finish(b, banks[r][:], r, engines[r])

        open_batch(0)
        flip_x1(0)
        regroup_x1(0)
        adp_grouped = flip(adp_sb)
        quantise_x1T(0)
        flip_wg(1)
        quantise(adp_codes[:], adp_scales[:], adp_grouped[:])
        quantise_stacks(0, 1, 1)
        flip_wg(0)
        quantise_wg(1)
        hop(0)
        regroup_h(0)
        quantise_wg(0)
        quantise_stacks(0, 0, 0)
        flip_wg(2, "VS")
        quantise_wg(2)
        flip_x1(1)
        quantise_x2(0)
        quantise_x1T(1)
        open_batch(1)
        regroup_h(1)
        regroup_x1(1)
        conv_x2_last(0, "SSSV")
        flip_x1(2)
        quantise_stacks(1, 0, 0)
        quantise_x1T(2)
        hop(1, "SSVS")
        quantise_stacks(1, 1, 1)
        flip_x1(3)
        quantise_x2(1)
        hop(2)
        open_batch(2)
        regroup_x1(2)
        regroup_h(2)
        quantise_x1T(3)
        quantise_stacks(2, 0, 1)
        quantise_x2(2)
        conv(1)

        for b in range(2, B):
            if b + 1 < B:
                open_batch(b + 1)
                regroup_x1(b + 1)
                regroup_h(b + 1)
            if b % 2 == 0:
                for later in range(b + 2, min(b + 4, B)):
                    flip_x1(later)
            if b + 2 < B:
                quantise_x1T(b + 2)
            if b + 1 < B:
                quantise_stacks(b + 1, 0, 1)
                hop(b + 1)
                quantise_x2(b + 1)
            conv(b, "SSSS" if b + 1 < B else "SVS")
        conv_last_rows(B - 1)
